import numpy as np
import ml_dtypes


def mxq(x, axis, fmt="e4m3"):
    dtype, down = {"e4m3": (ml_dtypes.float8_e4m3fn, 7), "e5m2": (ml_dtypes.float8_e5m2, 14)}[fmt]
    v = np.moveaxis(np.asarray(x, np.float32).astype(ml_dtypes.bfloat16).astype(np.float64), axis, -1)
    blocks = v.reshape(v.shape[:-1] + (-1, 32))
    amax = np.abs(blocks).max(-1, keepdims=True)
    byte = np.maximum(np.where(amax > 0, np.frexp(amax)[1] - 1 + 127, 0) - down, 1)
    scale = np.exp2(byte - 127.0)
    codes = (blocks / scale).astype(np.float32).astype(dtype).astype(np.float64)
    return np.moveaxis((codes * scale).reshape(v.shape), -1, axis)


BF16 = ml_dtypes.bfloat16


def bf(x):
    return np.asarray(x, np.float32).astype(BF16)


def f64(x):
    return np.asarray(x).astype(np.float64)


C_COUNT, NC, ROW, COL = 8, 48, 512, 512


def setup_inputs():
    z = np.random.standard_normal((C_COUNT, ROW, COL))
    load = np.random.standard_normal((C_COUNT, ROW, 1))
    pattern = np.random.standard_normal((C_COUNT, 1, COL))
    offset = np.random.standard_normal((C_COUNT, ROW, 1))
    gate = 1.0 + 0.375 * np.random.standard_normal((C_COUNT, ROW, 1))
    return {"feat_gated": bf(gate * (z + 0.7 * load * pattern + 0.5 * offset))}


def reference(feat_gated):
    F = f64(feat_gated)
    Fc = F - F.mean(-1, keepdims=True)
    inv_norm = 1.0 / np.sqrt((Fc * Fc).sum(-1, keepdims=True))
    Fn = Fc * inv_norm
    Fq = mxq(Fn, 2, "e4m3")
    return Fq @ Fq.transpose(0, 2, 1)

@@ -1,0 +1,167 @@
+from contextlib import ExitStack
+
+import concourse.masks as masks
+import concourse.mybir as mybir
+
+BF16 = mybir.dt.bfloat16
+F32 = mybir.dt.float32
+U32 = mybir.dt.uint32
+U8 = mybir.dt.uint8
+FP8X4 = mybir.dt.float8_e4m3fn_x4
+ALU = mybir.AluOpType
+ACT = mybir.ActivationFunctionType
+
+P = 128
+NCOM = 8
+ROWS = 512
+K = 512
+A = ROWS // P
+T = K // P
+FLOPS = 2 * NCOM * ROWS * ROWS * K
+
+PINNED = True
+
+
+def tile_generator_pb_kernel(tc, feat_gated, out):
+    nc = tc.nc
+    with ExitStack() as ctx:
+        const = ctx.enter_context(tc.tile_pool(name="const", bufs=1))
+        xin = ctx.enter_context(tc.tile_pool(name="xin", bufs=NCOM))
+        small = ctx.enter_context(tc.tile_pool(name="small", bufs=4))
+        fnp = ctx.enter_context(tc.tile_pool(name="fnp", bufs=3))
+        grp = ctx.enter_context(tc.tile_pool(name="grp", bufs=2))
+        cdp = ctx.enter_context(tc.tile_pool(name="cdp", bufs=2))
+        outp = ctx.enter_context(tc.tile_pool(name="outp", bufs=3))
+        ptr = ctx.enter_context(tc.psum_pool(name="ptr", bufs=4))
+        pmm = ctx.enter_context(tc.psum_pool(name="pmm", bufs=4))
+        if PINNED:
+            ctx.enter_context(tc.manual_schedule())
+
+        x = {}
+        mv = {}
+        inv = {}
+        fn = {}
+        xt = {}
+        grouped = {}
+        codes = {}
+        scales = {}
+        acc = {}
+        osb = {}
+
+        def ok(c):
+            return 0 <= c < NCOM
+
+        for c in range(NCOM):
+            x[c] = xin.tile([P, A, K], BF16, name="x")
+            nc.sync.dma_start(out=x[c][:], in_=feat_gated[c].rearrange("(p a) k -> p a k", a=A))
+
+        warm = const.tile([P, 1], F32, name="warm")
+        nc.vector.memset(warm[:], 1.0)
+        nc.scalar.activation(out=warm[:], in_=warm[:], func=ACT.Sqrt)
+        ident = const.tile([P, P], BF16, name="ident")
+        masks.make_identity(nc, ident[:])
+
+        def stats(c):
+            st6 = small.tile([P, A, 6], F32, name="st6")
+            mv[c] = small.tile([P, A, 2], F32, name="mv")
+            for a in range(A):
+                nc.vector.bn_stats(out=st6[:, a, :], in_=x[c][:, a, :])
+            for a in range(A):
+                nc.vector.bn_aggr(out=mv[c][:, a, :], in_=st6[:, a, :])
+
+        def norm_len(c):
+            nrm = small.tile([P, A, 1], F32, name="nrm")
+            nc.scalar.activation(out=nrm[:], in_=mv[c][:, :, 1:2], func=ACT.Sqrt, scale=float(K))
+            inv[c] = small.tile([P, A, 1], F32, name="inv")
+            nc.vector.reciprocal(out=inv[c][:], in_=nrm[:])
+
+        def normalise(c):
+            fn[c] = fnp.tile([P, A, K], BF16, name="fn")
+            for a in range(A):
+                nc.vector.tensor_scalar(
+                    out=fn[c][:, a, :], in0=x[c][:, a, :],
+                    scalar1=mv[c][:, a, 0:1], scalar2=inv[c][:, a, :],
+                    op0=ALU.subtract, op1=ALU.mult,
+                )
+
+        def transposes(c):
+            for a in range(A):
+                xt[c, a] = ptr.tile([P, T, P], BF16, name="xt")
+                for t in range(T):
+                    nc.tensor.transpose(xt[c, a][:, t, :], fn[c][:, a, t * P:(t + 1) * P], ident[:])
+
+        def regroup(c, a, eng):
+            if a == 0:
+                grouped[c] = grp.tile([P, A, P, T], BF16, name="grouped", align_bytes=64)
+            src = xt[c, a][:].rearrange("p t r -> p r t")
+            if eng == "S":
+                nc.scalar.copy(out=grouped[c][:, a, :, :], in_=src)
+            else:
+                nc.vector.tensor_copy(out=grouped[c][:, a, :, :], in_=src)
+
+        def quantise(c):
+            codes[c] = cdp.tile([P, ROWS], U32, name="codes", align_bytes=64)
+            scales[c] = cdp.tile([P, ROWS], U8, name="scales", align_bytes=64)
+            nc.vector.quantize_mx(
+                out=codes[c][:].bitcast(FP8X4), scales=scales[c][:],
+                in_=grouped[c][:].rearrange("p a r t -> p (a r t)"),
+            )
+
+        def products(c):
+            for a in range(A):
+                acc[c, a] = pmm.tile([P, ROWS], F32, name="acc")
+                cols = slice(a * P, (a + 1) * P)
+                nc.tensor.matmul_mx(
+                    out=acc[c, a][:],
+                    lhsT=codes[c][:, cols].bitcast(FP8X4), lhsT_scale=scales[c][:, cols],
+                    rhs=codes[c][:].bitcast(FP8X4), rhs_scale=scales[c][:],
+                    start=True, stop=True,
+                )
+
+        def evacuate(c, a, eng):
+            if a == 0:
+                osb[c] = outp.tile([P, A, ROWS], F32, name="osb")
+            dst = osb[c][:, a, :].rearrange("p (r b) -> p r b", b=A)
+            src = acc[c, a][:].rearrange("p (b r) -> p r b", b=A)
+            if eng == "S":
+                nc.scalar.copy(out=dst, in_=src)
+            else:
+                nc.vector.tensor_copy(out=dst, in_=src)
+
+        def store(c, a=None):
+            view = out[c].rearrange("(p a) n -> p a n", a=A)
+            if a is None:
+                nc.sync.dma_start(out=view, in_=osb[c][:])
+            else:
+                nc.sync.dma_start(out=view[:, a, :], in_=osb[c][:, a, :])
+
+        for s in range(NCOM + 2):
+            drain = s >= NCOM
+            if ok(s):
+                stats(s)
+            if ok(s - 1):
+                for a in range(A):
+                    regroup(s - 1, a, "V" if (drain and a >= 2) else "S")
+                quantise(s - 1)
+            if ok(s - 2):
+                evacuate(s - 2, 0, "S")
+            if ok(s):
+                norm_len(s)
+                normalise(s)
+                transposes(s)
+            if ok(s - 2):
+                fine = s - 2 == NCOM - 1
+                if fine:
+                    store(s - 2, 0)
+                for a in range(1, A):
+                    if drain:
+                        eng = "V" if a % 2 else "S"
+                    else:
+                        eng = "V" if (a == 3 and s % 2 == 0) else "S"
+                    evacuate(s - 2, a, eng)
+                    if fine:
+                        store(s - 2, a)
+                if not fine:
+                    store(s - 2)
+            if ok(s - 1):
+                products(s - 1)

@@ -19,41 +19,29 @@ A = ROWS // P
 T = K // P
 FLOPS = 2 * NCOM * ROWS * ROWS * K
 
-PINNED = True
-
 
 def tile_generator_pb_kernel(tc, feat_gated, out):
     nc = tc.nc
     with ExitStack() as ctx:
         const = ctx.enter_context(tc.tile_pool(name="const", bufs=1))
         xin = ctx.enter_context(tc.tile_pool(name="xin", bufs=NCOM))
-        small = ctx.enter_context(tc.tile_pool(name="small", bufs=4))
-        fnp = ctx.enter_context(tc.tile_pool(name="fnp", bufs=3))
-        grp = ctx.enter_context(tc.tile_pool(name="grp", bufs=2))
-        cdp = ctx.enter_context(tc.tile_pool(name="cdp", bufs=2))
-        outp = ctx.enter_context(tc.tile_pool(name="outp", bufs=3))
+        small = ctx.enter_context(tc.tile_pool(name="small", bufs=NCOM))
+        fnp = ctx.enter_context(tc.tile_pool(name="fnp", bufs=4))
+        grp = ctx.enter_context(tc.tile_pool(name="grp", bufs=3))
+        cdp = ctx.enter_context(tc.tile_pool(name="cdp", bufs=3))
+        outp = ctx.enter_context(tc.tile_pool(name="outp", bufs=4))
         ptr = ctx.enter_context(tc.psum_pool(name="ptr", bufs=4))
         pmm = ctx.enter_context(tc.psum_pool(name="pmm", bufs=4))
-        if PINNED:
-            ctx.enter_context(tc.manual_schedule())
 
         x = {}
-        mv = {}
-        inv = {}
-        fn = {}
-        xt = {}
-        grouped = {}
-        codes = {}
-        scales = {}
-        acc = {}
-        osb = {}
-
-        def ok(c):
-            return 0 <= c < NCOM
-
         for c in range(NCOM):
             x[c] = xin.tile([P, A, K], BF16, name="x")
-            nc.sync.dma_start(out=x[c][:], in_=feat_gated[c].rearrange("(p a) k -> p a k", a=A))
+            src = feat_gated[c].rearrange("(p a) k -> p a k", a=A)
+            if c < 1:
+                for a in range(A):
+                    nc.sync.dma_start(out=x[c][:, a, :], in_=src[:, a, :])
+            else:
+                nc.sync.dma_start(out=x[c][:], in_=src)
 
         warm = const.tile([P, 1], F32, name="warm")
         nc.vector.memset(warm[:], 1.0)
@@ -61,107 +49,50 @@ def tile_generator_pb_kernel(tc, feat_gated, out):
         ident = const.tile([P, P], BF16, name="ident")
         masks.make_identity(nc, ident[:])
 
-        def stats(c):
+        for c in range(NCOM):
             st6 = small.tile([P, A, 6], F32, name="st6")
-            mv[c] = small.tile([P, A, 2], F32, name="mv")
+            mv = small.tile([P, A, 2], F32, name="mv")
+            nrm = small.tile([P, A, 1], F32, name="nrm")
+            inv = small.tile([P, A, 1], F32, name="inv")
             for a in range(A):
                 nc.vector.bn_stats(out=st6[:, a, :], in_=x[c][:, a, :])
-            for a in range(A):
-                nc.vector.bn_aggr(out=mv[c][:, a, :], in_=st6[:, a, :])
-
-        def norm_len(c):
-            nrm = small.tile([P, A, 1], F32, name="nrm")
-            nc.scalar.activation(out=nrm[:], in_=mv[c][:, :, 1:2], func=ACT.Sqrt, scale=float(K))
-            inv[c] = small.tile([P, A, 1], F32, name="inv")
-            nc.vector.reciprocal(out=inv[c][:], in_=nrm[:])
-
-        def normalise(c):
-            fn[c] = fnp.tile([P, A, K], BF16, name="fn")
+                nc.vector.bn_aggr(out=mv[:, a, :], in_=st6[:, a, :])
+            nc.scalar.activation(out=nrm[:], in_=mv[:, :, 1:2], func=ACT.Sqrt, scale=float(K))
+            nc.vector.reciprocal(out=inv[:], in_=nrm[:])
+            fn = fnp.tile([P, A, K], BF16, name="fn")
+            grouped = grp.tile([P, A, P, T], BF16, name="grouped", align_bytes=64)
             for a in range(A):
                 nc.vector.tensor_scalar(
-                    out=fn[c][:, a, :], in0=x[c][:, a, :],
-                    scalar1=mv[c][:, a, 0:1], scalar2=inv[c][:, a, :],
+                    out=fn[:, a, :], in0=x[c][:, a, :],
+                    scalar1=mv[:, a, 0:1], scalar2=inv[:, a, :],
                     op0=ALU.subtract, op1=ALU.mult,
                 )
-
-        def transposes(c):
-            for a in range(A):
-                xt[c, a] = ptr.tile([P, T, P], BF16, name="xt")
+                xt = ptr.tile([P, T, P], BF16, name="xt")
                 for t in range(T):
-                    nc.tensor.transpose(xt[c, a][:, t, :], fn[c][:, a, t * P:(t + 1) * P], ident[:])
-
-        def regroup(c, a, eng):
-            if a == 0:
-                grouped[c] = grp.tile([P, A, P, T], BF16, name="grouped", align_bytes=64)
-            src = xt[c, a][:].rearrange("p t r -> p r t")
-            if eng == "S":
-                nc.scalar.copy(out=grouped[c][:, a, :, :], in_=src)
-            else:
-                nc.vector.tensor_copy(out=grouped[c][:, a, :, :], in_=src)
-
-        def quantise(c):
-            codes[c] = cdp.tile([P, ROWS], U32, name="codes", align_bytes=64)
-            scales[c] = cdp.tile([P, ROWS], U8, name="scales", align_bytes=64)
+                    nc.tensor.transpose(xt[:, t, :], fn[:, a, t * P:(t + 1) * P], ident[:])
+                nc.any.tensor_copy(out=grouped[:, a, :, :], in_=xt[:].rearrange("p t r -> p r t"))
+            codes = cdp.tile([P, ROWS], U32, name="codes", align_bytes=64)
+            scales = cdp.tile([P, ROWS], U8, name="scales", align_bytes=64)
             nc.vector.quantize_mx(
-                out=codes[c][:].bitcast(FP8X4), scales=scales[c][:],
-                in_=grouped[c][:].rearrange("p a r t -> p (a r t)"),
+                out=codes[:].bitcast(FP8X4), scales=scales[:],
+                in_=grouped[:].rearrange("p a r t -> p (a r t)"),
             )
-
-        def products(c):
+            osb = outp.tile([P, A, ROWS], F32, name="osb")
+            view = out[c].rearrange("(p a) n -> p a n", a=A)
             for a in range(A):
-                acc[c, a] = pmm.tile([P, ROWS], F32, name="acc")
+                acc = pmm.tile([P, ROWS], F32, name="acc")
                 cols = slice(a * P, (a + 1) * P)
                 nc.tensor.matmul_mx(
-                    out=acc[c, a][:],
-                    lhsT=codes[c][:, cols].bitcast(FP8X4), lhsT_scale=scales[c][:, cols],
-                    rhs=codes[c][:].bitcast(FP8X4), rhs_scale=scales[c][:],
+                    out=acc[:],
+                    lhsT=codes[:, cols].bitcast(FP8X4), lhsT_scale=scales[:, cols],
+                    rhs=codes[:].bitcast(FP8X4), rhs_scale=scales[:],
                     start=True, stop=True,
                 )
-
-        def evacuate(c, a, eng):
-            if a == 0:
-                osb[c] = outp.tile([P, A, ROWS], F32, name="osb")
-            dst = osb[c][:, a, :].rearrange("p (r b) -> p r b", b=A)
-            src = acc[c, a][:].rearrange("p (b r) -> p r b", b=A)
-            if eng == "S":
-                nc.scalar.copy(out=dst, in_=src)
-            else:
-                nc.vector.tensor_copy(out=dst, in_=src)
-
-        def store(c, a=None):
-            view = out[c].rearrange("(p a) n -> p a n", a=A)
-            if a is None:
-                nc.sync.dma_start(out=view, in_=osb[c][:])
-            else:
-                nc.sync.dma_start(out=view[:, a, :], in_=osb[c][:, a, :])
-
-        for s in range(NCOM + 2):
-            drain = s >= NCOM
-            if ok(s):
-                stats(s)
-            if ok(s - 1):
-                for a in range(A):
-                    regroup(s - 1, a, "V" if (drain and a >= 2) else "S")
-                quantise(s - 1)
-            if ok(s - 2):
-                evacuate(s - 2, 0, "S")
-            if ok(s):
-                norm_len(s)
-                normalise(s)
-                transposes(s)
-            if ok(s - 2):
-                fine = s - 2 == NCOM - 1
-                if fine:
-                    store(s - 2, 0)
-                for a in range(1, A):
-                    if drain:
-                        eng = "V" if a % 2 else "S"
-                    else:
-                        eng = "V" if (a == 3 and s % 2 == 0) else "S"
-                    evacuate(s - 2, a, eng)
-                    if fine:
-                        store(s - 2, a)
-                if not fine:
-                    store(s - 2)
-            if ok(s - 1):
-                products(s - 1)
+                nc.any.tensor_copy(
+                    out=osb[:, a, :].rearrange("p (r b) -> p r b", b=A),
+                    in_=acc[:].rearrange("p (b r) -> p r b", b=A),
+                )
+                if c >= NCOM - 2:
+                    nc.sync.dma_start(out=view[:, a, :], in_=osb[:, a, :])
+            if c < NCOM - 2:
+                nc.sync.dma_start(out=view, in_=osb[:])

@@ -27,11 +27,18 @@ def tile_generator_pb_kernel(tc, feat_gated, out):
         xin = ctx.enter_context(tc.tile_pool(name="xin", bufs=NCOM))
         small = ctx.enter_context(tc.tile_pool(name="small", bufs=NCOM))
         fnp = ctx.enter_context(tc.tile_pool(name="fnp", bufs=4))
+        plp = ctx.enter_context(tc.tile_pool(name="plp", bufs=6))
         grp = ctx.enter_context(tc.tile_pool(name="grp", bufs=3))
         cdp = ctx.enter_context(tc.tile_pool(name="cdp", bufs=3))
         outp = ctx.enter_context(tc.tile_pool(name="outp", bufs=4))
         ptr = ctx.enter_context(tc.psum_pool(name="ptr", bufs=4))
         pmm = ctx.enter_context(tc.psum_pool(name="pmm", bufs=4))
+
+        def copy_out(on_vector, dst, src_psum):
+            if on_vector:
+                nc.vector.tensor_copy(out=dst, in_=src_psum)
+            else:
+                nc.scalar.copy(out=dst, in_=src_psum)
 
         x = {}
         for c in range(NCOM):
@@ -56,6 +63,7 @@ def tile_generator_pb_kernel(tc, feat_gated, out):
             inv = small.tile([P, A, 1], F32, name="inv")
             for a in range(A):
                 nc.vector.bn_stats(out=st6[:, a, :], in_=x[c][:, a, :])
+            for a in range(A):
                 nc.vector.bn_aggr(out=mv[:, a, :], in_=st6[:, a, :])
             nc.scalar.activation(out=nrm[:], in_=mv[:, :, 1:2], func=ACT.Sqrt, scale=float(K))
             nc.vector.reciprocal(out=inv[:], in_=nrm[:])
@@ -67,10 +75,19 @@ def tile_generator_pb_kernel(tc, feat_gated, out):
                     scalar1=mv[:, a, 0:1], scalar2=inv[:, a, :],
                     op0=ALU.subtract, op1=ALU.mult,
                 )
+            for a in range(A):
                 xt = ptr.tile([P, T, P], BF16, name="xt")
                 for t in range(T):
                     nc.tensor.transpose(xt[:, t, :], fn[:, a, t * P:(t + 1) * P], ident[:])
-                nc.any.tensor_copy(out=grouped[:, a, :, :], in_=xt[:].rearrange("p t r -> p r t"))
+                if a < 3:
+                    planes = plp.tile([P, T, P], BF16, name="planes")
+                    nc.scalar.copy(out=planes[:], in_=xt[:])
+                    nc.gpsimd.tensor_scalar(
+                        out=grouped[:, a, :, :], in0=planes[:].rearrange("p t r -> p r t"),
+                        scalar1=1.0, scalar2=0.0, op0=ALU.mult, op1=ALU.add,
+                    )
+                else:
+                    copy_out(False, grouped[:, a, :, :], xt[:].rearrange("p t r -> p r t"))
             codes = cdp.tile([P, ROWS], U32, name="codes", align_bytes=64)
             scales = cdp.tile([P, ROWS], U8, name="scales", align_bytes=64)
             nc.vector.quantize_mx(
@@ -88,11 +105,12 @@ def tile_generator_pb_kernel(tc, feat_gated, out):
                     rhs=codes[:].bitcast(FP8X4), rhs_scale=scales[:],
                     start=True, stop=True,
                 )
-                nc.any.tensor_copy(
-                    out=osb[:, a, :].rearrange("p (r b) -> p r b", b=A),
-                    in_=acc[:].rearrange("p (b r) -> p r b", b=A),
+                copy_out(
+                    (a == 3 and c >= 3) or (a == 1 and c >= 6),
+                    osb[:, a, :].rearrange("p (r b) -> p r b", b=A),
+                    acc[:].rearrange("p (b r) -> p r b", b=A),
                 )
-                if c >= NCOM - 2:
+                if c >= NCOM - 3:
                     nc.sync.dma_start(out=view[:, a, :], in_=osb[:, a, :])
-            if c < NCOM - 2:
+            if c < NCOM - 3:
                 nc.sync.dma_start(out=view, in_=osb[:])

@@ -17,6 +17,7 @@ ROWS = 512
 K = 512
 A = ROWS // P
 T = K // P
+NT = NCOM * A
 FLOPS = 2 * NCOM * ROWS * ROWS * K
 
 
@@ -27,24 +28,34 @@ def tile_generator_pb_kernel(tc, feat_gated, out):
         xin = ctx.enter_context(tc.tile_pool(name="xin", bufs=NCOM))
         small = ctx.enter_context(tc.tile_pool(name="small", bufs=NCOM))
         fnp = ctx.enter_context(tc.tile_pool(name="fnp", bufs=4))
-        plp = ctx.enter_context(tc.tile_pool(name="plp", bufs=6))
-        grp = ctx.enter_context(tc.tile_pool(name="grp", bufs=3))
-        cdp = ctx.enter_context(tc.tile_pool(name="cdp", bufs=3))
-        outp = ctx.enter_context(tc.tile_pool(name="outp", bufs=4))
+        grp = ctx.enter_context(tc.tile_pool(name="grp", bufs=2))
+        cdp = ctx.enter_context(tc.tile_pool(name="cdp", bufs=2))
+        outp = ctx.enter_context(tc.tile_pool(name="outp", bufs=3))
         ptr = ctx.enter_context(tc.psum_pool(name="ptr", bufs=4))
         pmm = ctx.enter_context(tc.psum_pool(name="pmm", bufs=4))
-
-        def copy_out(on_vector, dst, src_psum):
-            if on_vector:
-                nc.vector.tensor_copy(out=dst, in_=src_psum)
-            else:
-                nc.scalar.copy(out=dst, in_=src_psum)
+        ctx.enter_context(tc.manual_schedule())
 
         x = {}
+        st6 = {}
+        mv = {}
+        nrm = {}
+        inv = {}
+        fn = {}
+        xt = {}
+        grouped = {}
+        codes = {}
+        scales = {}
+        acc = {}
+        osb = {}
+        stream = {"next": 0}
+
+        def ok(c):
+            return 0 <= c < NCOM
+
         for c in range(NCOM):
             x[c] = xin.tile([P, A, K], BF16, name="x")
             src = feat_gated[c].rearrange("(p a) k -> p a k", a=A)
-            if c < 1:
+            if c == 0:
                 for a in range(A):
                     nc.sync.dma_start(out=x[c][:, a, :], in_=src[:, a, :])
             else:
@@ -56,61 +67,136 @@ def tile_generator_pb_kernel(tc, feat_gated, out):
         ident = const.tile([P, P], BF16, name="ident")
         masks.make_identity(nc, ident[:])
 
-        for c in range(NCOM):
-            st6 = small.tile([P, A, 6], F32, name="st6")
-            mv = small.tile([P, A, 2], F32, name="mv")
-            nrm = small.tile([P, A, 1], F32, name="nrm")
-            inv = small.tile([P, A, 1], F32, name="inv")
-            for a in range(A):
-                nc.vector.bn_stats(out=st6[:, a, :], in_=x[c][:, a, :])
-            for a in range(A):
-                nc.vector.bn_aggr(out=mv[:, a, :], in_=st6[:, a, :])
-            nc.scalar.activation(out=nrm[:], in_=mv[:, :, 1:2], func=ACT.Sqrt, scale=float(K))
-            nc.vector.reciprocal(out=inv[:], in_=nrm[:])
-            fn = fnp.tile([P, A, K], BF16, name="fn")
-            grouped = grp.tile([P, A, P, T], BF16, name="grouped", align_bytes=64)
+        def unit():
+            m = stream["next"]
+            if m < NT:
+                c, a = divmod(m, A)
+                if a == 0:
+                    st6[c] = small.tile([P, A, 6], F32, name="st6")
+                    mv[c] = small.tile([P, A, 2], F32, name="mv")
+                nc.vector.bn_stats(out=st6[c][:, a, :], in_=x[c][:, a, :])
+            if 1 <= m <= NT:
+                c, a = divmod(m - 1, A)
+                nc.vector.bn_aggr(out=mv[c][:, a, :], in_=st6[c][:, a, :])
+            stream["next"] = m + 1
+
+        def stats_through(c):
+            while stream["next"] <= A * c + A:
+                unit()
+
+        def filler():
+            if stream["next"] <= NT:
+                unit()
+
+        def root(c):
+            nrm[c] = small.tile([P, A, 1], F32, name="nrm")
+            nc.scalar.activation(out=nrm[c][:], in_=mv[c][:, :, 1:2], func=ACT.Sqrt, scale=float(K))
+
+        def recip(c):
+            inv[c] = small.tile([P, A, 1], F32, name="inv")
+            nc.vector.reciprocal(out=inv[c][:], in_=nrm[c][:])
+
+        def normalise(c):
+            fn[c] = fnp.tile([P, A, K], BF16, name="fn")
             for a in range(A):
                 nc.vector.tensor_scalar(
-                    out=fn[:, a, :], in0=x[c][:, a, :],
-                    scalar1=mv[:, a, 0:1], scalar2=inv[:, a, :],
+                    out=fn[c][:, a, :], in0=x[c][:, a, :],
+                    scalar1=mv[c][:, a, 0:1], scalar2=inv[c][:, a, :],
                     op0=ALU.subtract, op1=ALU.mult,
                 )
-            for a in range(A):
-                xt = ptr.tile([P, T, P], BF16, name="xt")
-                for t in range(T):
-                    nc.tensor.transpose(xt[:, t, :], fn[:, a, t * P:(t + 1) * P], ident[:])
-                if a < 3:
-                    planes = plp.tile([P, T, P], BF16, name="planes")
-                    nc.scalar.copy(out=planes[:], in_=xt[:])
-                    nc.gpsimd.tensor_scalar(
-                        out=grouped[:, a, :, :], in0=planes[:].rearrange("p t r -> p r t"),
-                        scalar1=1.0, scalar2=0.0, op0=ALU.mult, op1=ALU.add,
-                    )
-                else:
-                    copy_out(False, grouped[:, a, :, :], xt[:].rearrange("p t r -> p r t"))
-            codes = cdp.tile([P, ROWS], U32, name="codes", align_bytes=64)
-            scales = cdp.tile([P, ROWS], U8, name="scales", align_bytes=64)
+
+        def transposes(c, a):
+            xt[c, a] = ptr.tile([P, T, P], BF16, name="xt")
+            for t in range(T):
+                nc.tensor.transpose(xt[c, a][:, t, :], fn[c][:, a, t * P:(t + 1) * P], ident[:])
+
+        def copy_out(on_vector, dst, src_psum):
+            if on_vector:
+                nc.vector.tensor_copy(out=dst, in_=src_psum)
+            else:
+                nc.scalar.copy(out=dst, in_=src_psum)
+
+        def regroup(c, a):
+            if a == 0:
+                grouped[c] = grp.tile([P, A, P, T], BF16, name="grouped", align_bytes=64)
+            copy_out((a == 3 and c >= 6) or (a == 2 and c >= 7), grouped[c][:, a, :, :], xt[c, a][:].rearrange("p t r -> p r t"))
+
+        def quantise(c):
+            codes[c] = cdp.tile([P, ROWS], U32, name="codes", align_bytes=64)
+            scales[c] = cdp.tile([P, ROWS], U8, name="scales", align_bytes=64)
             nc.vector.quantize_mx(
-                out=codes[:].bitcast(FP8X4), scales=scales[:],
-                in_=grouped[:].rearrange("p a r t -> p (a r t)"),
+                out=codes[c][:].bitcast(FP8X4), scales=scales[c][:],
+                in_=grouped[c][:].rearrange("p a r t -> p (a r t)"),
             )
-            osb = outp.tile([P, A, ROWS], F32, name="osb")
+
+        def product(c, a):
+            acc[c, a] = pmm.tile([P, ROWS], F32, name="acc")
+            cols = slice(a * P, (a + 1) * P)
+            nc.tensor.matmul_mx(
+                out=acc[c, a][:],
+                lhsT=codes[c][:, cols].bitcast(FP8X4), lhsT_scale=scales[c][:, cols],
+                rhs=codes[c][:].bitcast(FP8X4), rhs_scale=scales[c][:],
+                start=True, stop=True,
+            )
+
+        def ev_on_vector(c, a):
+            return (a == 3 and c >= 1) or (a == 1 and c >= 6)
+
+        def evacuate(c, a):
+            copy_out(
+                ev_on_vector(c, a),
+                osb[c][:, a, :].rearrange("p (r b) -> p r b", b=A),
+                acc[c, a][:].rearrange("p (b r) -> p r b", b=A),
+            )
+
+        def store(c):
             view = out[c].rearrange("(p a) n -> p a n", a=A)
-            for a in range(A):
-                acc = pmm.tile([P, ROWS], F32, name="acc")
-                cols = slice(a * P, (a + 1) * P)
-                nc.tensor.matmul_mx(
-                    out=acc[:],
-                    lhsT=codes[:, cols].bitcast(FP8X4), lhsT_scale=scales[:, cols],
-                    rhs=codes[:].bitcast(FP8X4), rhs_scale=scales[:],
-                    start=True, stop=True,
-                )
-                copy_out(
-                    (a == 3 and c >= 3) or (a == 1 and c >= 6),
-                    osb[:, a, :].rearrange("p (r b) -> p r b", b=A),
-                    acc[:].rearrange("p (b r) -> p r b", b=A),
-                )
-                if c >= NCOM - 3:
-                    nc.sync.dma_start(out=view[:, a, :], in_=osb[:, a, :])
-            if c < NCOM - 3:
-                nc.sync.dma_start(out=view, in_=osb[:])
+            if c >= NCOM - 3:
+                for a in range(A):
+                    nc.sync.dma_start(out=view[:, a, :], in_=osb[c][:, a, :])
+            else:
+                nc.sync.dma_start(out=view, in_=osb[c][:])
+
+        stats_through(0)
+        root(0)
+        filler()
+        recip(0)
+        filler()
+        normalise(0)
+        for a in range(A):
+            transposes(0, a)
+
+        for p in range(-1, NCOM + 1):
+            if ok(p):
+                for a in range(A):
+                    regroup(p, a)
+                    if ok(p + 1):
+                        transposes(p + 1, a)
+            if ok(p + 2):
+                stats_through(p + 2)
+            if ok(p - 1):
+                osb[p - 1] = outp.tile([P, A, ROWS], F32, name="osb")
+                for a in range(A):
+                    if ev_on_vector(p - 1, a):
+                        evacuate(p - 1, a)
+            if ok(p):
+                quantise(p)
+            rooted = not ok(p + 2)
+            if ok(p - 1):
+                for a in range(A):
+                    if not ev_on_vector(p - 1, a):
+                        evacuate(p - 1, a)
+                        if not rooted:
+                            root(p + 2)
+                            rooted = True
+            if not rooted:
+                root(p + 2)
+            if ok(p - 1):
+                store(p - 1)
+            if ok(p + 2):
+                recip(p + 2)
+                filler()
+                normalise(p + 2)
+            if ok(p):
+                for a in range(A):
+                    product(p, a)

@@ -17,8 +17,11 @@ ROWS = 512
 K = 512
 A = ROWS // P
 T = K // P
-NT = NCOM * A
 FLOPS = 2 * NCOM * ROWS * ROWS * K
+
+
+def stats_on_scalar(c, a):
+    return a == 3 and c <= 1
 
 
 def tile_generator_pb_kernel(tc, feat_gated, out):
@@ -27,6 +30,7 @@ def tile_generator_pb_kernel(tc, feat_gated, out):
         const = ctx.enter_context(tc.tile_pool(name="const", bufs=1))
         xin = ctx.enter_context(tc.tile_pool(name="xin", bufs=NCOM))
         small = ctx.enter_context(tc.tile_pool(name="small", bufs=NCOM))
+        junkp = ctx.enter_context(tc.tile_pool(name="junkp", bufs=2))
         fnp = ctx.enter_context(tc.tile_pool(name="fnp", bufs=4))
         grp = ctx.enter_context(tc.tile_pool(name="grp", bufs=2))
         cdp = ctx.enter_context(tc.tile_pool(name="cdp", bufs=2))
@@ -38,6 +42,8 @@ def tile_generator_pb_kernel(tc, feat_gated, out):
         x = {}
         st6 = {}
         mv = {}
+        smean = {}
+        ssq = {}
         nrm = {}
         inv = {}
         fn = {}
@@ -47,7 +53,12 @@ def tile_generator_pb_kernel(tc, feat_gated, out):
         scales = {}
         acc = {}
         osb = {}
+        regrouped = set()
         stream = {"next": 0}
+        vector_tiles = [(c, a) for c in range(NCOM) for a in range(A) if not stats_on_scalar(c, a)]
+        last_of = {}
+        for i, (c, a) in enumerate(vector_tiles):
+            last_of[c] = i
 
         def ok(c):
             return 0 <= c < NCOM
@@ -60,6 +71,8 @@ def tile_generator_pb_kernel(tc, feat_gated, out):
                     nc.sync.dma_start(out=x[c][:, a, :], in_=src[:, a, :])
             else:
                 nc.sync.dma_start(out=x[c][:], in_=src)
+            st6[c] = small.tile([P, A, 6], F32, name="st6")
+            mv[c] = small.tile([P, A, 2], F32, name="mv")
 
         warm = const.tile([P, 1], F32, name="warm")
         nc.vector.memset(warm[:], 1.0)
@@ -69,28 +82,45 @@ def tile_generator_pb_kernel(tc, feat_gated, out):
 
         def unit():
             m = stream["next"]
-            if m < NT:
-                c, a = divmod(m, A)
-                if a == 0:
-                    st6[c] = small.tile([P, A, 6], F32, name="st6")
-                    mv[c] = small.tile([P, A, 2], F32, name="mv")
+            if m < len(vector_tiles):
+                c, a = vector_tiles[m]
                 nc.vector.bn_stats(out=st6[c][:, a, :], in_=x[c][:, a, :])
-            if 1 <= m <= NT:
-                c, a = divmod(m - 1, A)
+            if 1 <= m <= len(vector_tiles):
+                c, a = vector_tiles[m - 1]
                 nc.vector.bn_aggr(out=mv[c][:, a, :], in_=st6[c][:, a, :])
             stream["next"] = m + 1
 
         def stats_through(c):
-            while stream["next"] <= A * c + A:
+            while stream["next"] <= last_of[c] + 1:
                 unit()
 
         def filler():
-            if stream["next"] <= NT:
+            if stream["next"] <= len(vector_tiles):
                 unit()
+
+        def scalar_mean(c, a):
+            smean[c, a] = small.tile([P, 1], F32, name="smean")
+            junk = junkp.tile([P, K], BF16, name="junk")
+            nc.scalar.activation(
+                out=junk[:], in_=x[c][:, a, :], func=ACT.Identity, scale=1.0 / K, accum_out=smean[c, a][:]
+            )
+
+        def scalar_sumsq(c, a):
+            ssq[c, a] = small.tile([P, 1], F32, name="ssq")
+            junk = junkp.tile([P, K], BF16, name="junk")
+            nc.scalar.activation(
+                out=junk[:], in_=x[c][:, a, :], func=ACT.Square, scale=-1.0, bias=smean[c, a][:],
+                accum_out=ssq[c, a][:],
+            )
 
         def root(c):
             nrm[c] = small.tile([P, A, 1], F32, name="nrm")
-            nc.scalar.activation(out=nrm[c][:], in_=mv[c][:, :, 1:2], func=ACT.Sqrt, scale=float(K))
+            on_v = [a for a in range(A) if not stats_on_scalar(c, a)]
+            lo, hi = on_v[0], on_v[-1] + 1
+            nc.scalar.activation(out=nrm[c][:, lo:hi, :], in_=mv[c][:, lo:hi, 1:2], func=ACT.Sqrt, scale=float(K))
+            for a in range(A):
+                if stats_on_scalar(c, a):
+                    nc.scalar.activation(out=nrm[c][:, a, :], in_=ssq[c, a][:], func=ACT.Sqrt)
 
         def recip(c):
             inv[c] = small.tile([P, A, 1], F32, name="inv")
@@ -99,9 +129,10 @@ def tile_generator_pb_kernel(tc, feat_gated, out):
         def normalise(c):
             fn[c] = fnp.tile([P, A, K], BF16, name="fn")
             for a in range(A):
+                mean = smean[c, a][:] if stats_on_scalar(c, a) else mv[c][:, a, 0:1]
                 nc.vector.tensor_scalar(
                     out=fn[c][:, a, :], in0=x[c][:, a, :],
-                    scalar1=mv[c][:, a, 0:1], scalar2=inv[c][:, a, :],
+                    scalar1=mean, scalar2=inv[c][:, a, :],
                     op0=ALU.subtract, op1=ALU.mult,
                 )
 
@@ -117,6 +148,9 @@ def tile_generator_pb_kernel(tc, feat_gated, out):
                 nc.scalar.copy(out=dst, in_=src_psum)
 
         def regroup(c, a):
+            if (c, a) in regrouped:
+                return
+            regrouped.add((c, a))
             if a == 0:
                 grouped[c] = grp.tile([P, A, P, T], BF16, name="grouped", align_bytes=64)
             copy_out((a == 3 and c >= 6) or (a == 2 and c >= 7), grouped[c][:, a, :, :], xt[c, a][:].rearrange("p t r -> p r t"))
@@ -157,8 +191,18 @@ def tile_generator_pb_kernel(tc, feat_gated, out):
             else:
                 nc.sync.dma_start(out=view, in_=osb[c][:])
 
+        def scalar_stats(c):
+            for a in range(A):
+                if stats_on_scalar(c, a):
+                    scalar_mean(c, a)
+            for a in range(A):
+                if stats_on_scalar(c, a):
+                    scalar_sumsq(c, a)
+
+        scalar_stats(0)
         stats_through(0)
         root(0)
+        scalar_stats(1)
         filler()
         recip(0)
         filler()
@@ -167,6 +211,9 @@ def tile_generator_pb_kernel(tc, feat_gated, out):
             transposes(0, a)
 
         for p in range(-1, NCOM + 1):
+            if p == -1:
+                for a in range(0):
+                    regroup(0, a)
             if ok(p):
                 for a in range(A):
                     regroup(p, a)
@@ -174,12 +221,15 @@ def tile_generator_pb_kernel(tc, feat_gated, out):
                         transposes(p + 1, a)
             if ok(p + 2):
                 stats_through(p + 2)
+            late = False
+            if late and ok(p):
+                quantise(p)
             if ok(p - 1):
                 osb[p - 1] = outp.tile([P, A, ROWS], F32, name="osb")
                 for a in range(A):
                     if ev_on_vector(p - 1, a):
                         evacuate(p - 1, a)
-            if ok(p):
+            if ok(p) and not late:
                 quantise(p)
             rooted = not ok(p + 2)
             if ok(p - 1):

@@ -231,6 +231,8 @@ def tile_generator_pb_kernel(tc, feat_gated, out):
                         evacuate(p - 1, a)
             if ok(p) and not late:
                 quantise(p)
+            if ok(p + 2):
+                filler()
             rooted = not ok(p + 2)
             if ok(p - 1):
                 for a in range(A):

@@ -44,7 +44,6 @@ def tile_generator_pb_kernel(tc, feat_gated, out):
         mv = {}
         smean = {}
         ssq = {}
-        nrm = {}
         inv = {}
         fn = {}
         xt = {}
@@ -53,7 +52,6 @@ def tile_generator_pb_kernel(tc, feat_gated, out):
         scales = {}
         acc = {}
         osb = {}
-        regrouped = set()
         stream = {"next": 0}
         vector_tiles = [(c, a) for c in range(NCOM) for a in range(A) if not stats_on_scalar(c, a)]
         last_of = {}
@@ -76,8 +74,8 @@ def tile_generator_pb_kernel(tc, feat_gated, out):
 
         warm = const.tile([P, 1], F32, name="warm")
         nc.vector.memset(warm[:], 1.0)
-        nc.scalar.activation(out=warm[:], in_=warm[:], func=ACT.Sqrt)
-        ident = const.tile([P, P], BF16, name="ident")
+        nc.scalar.activation(out=warm[:], in_=warm[:], func=ACT.Abs_reciprocal_sqrt)
+        ident = const.tile([P, P], F32, name="ident")
         masks.make_identity(nc, ident[:])
 
         def unit():
@@ -114,17 +112,13 @@ def tile_generator_pb_kernel(tc, feat_gated, out):
             )
 
         def root(c):
-            nrm[c] = small.tile([P, A, 1], F32, name="nrm")
+            inv[c] = small.tile([P, A, 1], F32, name="inv")
             on_v = [a for a in range(A) if not stats_on_scalar(c, a)]
             lo, hi = on_v[0], on_v[-1] + 1
-            nc.scalar.activation(out=nrm[c][:, lo:hi, :], in_=mv[c][:, lo:hi, 1:2], func=ACT.Sqrt, scale=float(K))
+            nc.scalar.activation(out=inv[c][:, lo:hi, :], in_=mv[c][:, lo:hi, 1:2], func=ACT.Abs_reciprocal_sqrt, scale=float(K))
             for a in range(A):
                 if stats_on_scalar(c, a):
-                    nc.scalar.activation(out=nrm[c][:, a, :], in_=ssq[c, a][:], func=ACT.Sqrt)
-
-        def recip(c):
-            inv[c] = small.tile([P, A, 1], F32, name="inv")
-            nc.vector.reciprocal(out=inv[c][:], in_=nrm[c][:])
+                    nc.scalar.activation(out=inv[c][:, a, :], in_=ssq[c, a][:], func=ACT.Abs_reciprocal_sqrt)
 
         def normalise(c):
             fn[c] = fnp.tile([P, A, K], BF16, name="fn")
@@ -136,10 +130,12 @@ def tile_generator_pb_kernel(tc, feat_gated, out):
                     op0=ALU.subtract, op1=ALU.mult,
                 )
 
-        def transposes(c, a):
-            xt[c, a] = ptr.tile([P, T, P], BF16, name="xt")
-            for t in range(T):
-                nc.tensor.transpose(xt[c, a][:, t, :], fn[c][:, a, t * P:(t + 1) * P], ident[:])
+        def transposes(c, h):
+            xt[c, h] = ptr.tile([P, 2, 2, P], F32, name="xt")
+            for i in range(2):
+                words = fn[c][:, 2 * h + i, :].bitcast(F32)
+                for u in range(2):
+                    nc.tensor.transpose(xt[c, h][:, i, u, :], words[:, u:2 * P:2], ident[:])
 
         def copy_out(on_vector, dst, src_psum):
             if on_vector:
@@ -147,13 +143,14 @@ def tile_generator_pb_kernel(tc, feat_gated, out):
             else:
                 nc.scalar.copy(out=dst, in_=src_psum)
 
-        def regroup(c, a):
-            if (c, a) in regrouped:
-                return
-            regrouped.add((c, a))
-            if a == 0:
+        def regroup(c, h):
+            if h == 0:
                 grouped[c] = grp.tile([P, A, P, T], BF16, name="grouped", align_bytes=64)
-            copy_out((a == 3 and c >= 6) or (a == 2 and c >= 7), grouped[c][:, a, :, :], xt[c, a][:].rearrange("p t r -> p r t"))
+            copy_out(
+                h == 1 and c >= 7,
+                grouped[c][:, 2 * h:2 * h + 2, :, :].bitcast(F32),
+                xt[c, h][:].rearrange("p a u r -> p a r u"),
+            )
 
         def quantise(c):
             codes[c] = cdp.tile([P, ROWS], U32, name="codes", align_bytes=64)
@@ -174,7 +171,7 @@ def tile_generator_pb_kernel(tc, feat_gated, out):
             )
 
         def ev_on_vector(c, a):
-            return (a == 3 and c >= 1) or (a == 1 and c >= 6)
+            return a % 2 == 1 and c >= 6
 
         def evacuate(c, a):
             copy_out(
@@ -204,32 +201,25 @@ def tile_generator_pb_kernel(tc, feat_gated, out):
         root(0)
         scalar_stats(1)
         filler()
-        recip(0)
         filler()
         normalise(0)
-        for a in range(A):
-            transposes(0, a)
+        for h in range(2):
+            transposes(0, h)
 
         for p in range(-1, NCOM + 1):
-            if p == -1:
-                for a in range(0):
-                    regroup(0, a)
             if ok(p):
-                for a in range(A):
-                    regroup(p, a)
+                for h in range(2):
+                    regroup(p, h)
                     if ok(p + 1):
-                        transposes(p + 1, a)
+                        transposes(p + 1, h)
             if ok(p + 2):
                 stats_through(p + 2)
-            late = False
-            if late and ok(p):
-                quantise(p)
             if ok(p - 1):
                 osb[p - 1] = outp.tile([P, A, ROWS], F32, name="osb")
                 for a in range(A):
                     if ev_on_vector(p - 1, a):
                         evacuate(p - 1, a)
-            if ok(p) and not late:
+            if ok(p):
                 quantise(p)
             if ok(p + 2):
                 filler()
@@ -246,7 +236,6 @@ def tile_generator_pb_kernel(tc, feat_gated, out):
             if ok(p - 1):
                 store(p - 1)
             if ok(p + 2):
-                recip(p + 2)
                 filler()
                 normalise(p + 2)
             if ok(p):

@@ -24,6 +24,10 @@ def stats_on_scalar(c, a):
     return a == 3 and c <= 1
 
 
+def norm_on_gpsimd(c, a):
+    return c >= 2 and a >= 2
+
+
 def tile_generator_pb_kernel(tc, feat_gated, out):
     nc = tc.nc
     with ExitStack() as ctx:
@@ -124,11 +128,21 @@ def tile_generator_pb_kernel(tc, feat_gated, out):
             fn[c] = fnp.tile([P, A, K], BF16, name="fn")
             for a in range(A):
                 mean = smean[c, a][:] if stats_on_scalar(c, a) else mv[c][:, a, 0:1]
-                nc.vector.tensor_scalar(
-                    out=fn[c][:, a, :], in0=x[c][:, a, :],
-                    scalar1=mean, scalar2=inv[c][:, a, :],
-                    op0=ALU.subtract, op1=ALU.mult,
-                )
+                if norm_on_gpsimd(c, a):
+                    shift = small.tile([P, 1], F32, name="shift", bufs=4)
+                    nc.gpsimd.tensor_scalar(
+                        out=shift[:], in0=mean, scalar1=inv[c][:, a, :], scalar2=-1.0, op0=ALU.mult, op1=ALU.mult
+                    )
+                    nc.gpsimd.tensor_scalar(
+                        out=fn[c][:, a, :], in0=x[c][:, a, :],
+                        scalar1=inv[c][:, a, :], scalar2=shift[:], op0=ALU.mult, op1=ALU.add,
+                    )
+                else:
+                    nc.vector.tensor_scalar(
+                        out=fn[c][:, a, :], in0=x[c][:, a, :],
+                        scalar1=mean, scalar2=inv[c][:, a, :],
+                        op0=ALU.subtract, op1=ALU.mult,
+                    )
 
         def transposes(c, h):
             xt[c, h] = ptr.tile([P, 2, 2, P], F32, name="xt")

@@ -21,7 +21,7 @@ FLOPS = 2 * NCOM * ROWS * ROWS * K
 
 
 def stats_on_scalar(c, a):
-    return a == 3 and c <= 1
+    return a == 3 and c <= 3
 
 
 def norm_on_gpsimd(c, a):
@@ -185,7 +185,7 @@ def tile_generator_pb_kernel(tc, feat_gated, out):
             )
 
         def ev_on_vector(c, a):
-            return a % 2 == 1 and c >= 6
+            return a % 2 == 1 and c >= 5
 
         def evacuate(c, a):
             copy_out(
@@ -214,6 +214,7 @@ def tile_generator_pb_kernel(tc, feat_gated, out):
         stats_through(0)
         root(0)
         scalar_stats(1)
+        scalar_stats(2)
         filler()
         filler()
         normalise(0)
@@ -226,6 +227,8 @@ def tile_generator_pb_kernel(tc, feat_gated, out):
                     regroup(p, h)
                     if ok(p + 1):
                         transposes(p + 1, h)
+            if 0 <= p and ok(p + 3):
+                scalar_stats(p + 3)
             if ok(p + 2):
                 stats_through(p + 2)
             if ok(p - 1):

@@ -25,7 +25,7 @@ def stats_on_scalar(c, a):
 
 
 def norm_on_gpsimd(c, a):
-    return c >= 2 and a >= 2
+    return 2 <= c <= 6 and a >= 2
 
 
 def tile_generator_pb_kernel(tc, feat_gated, out):
@@ -39,8 +39,8 @@ def tile_generator_pb_kernel(tc, feat_gated, out):
         grp = ctx.enter_context(tc.tile_pool(name="grp", bufs=2))
         cdp = ctx.enter_context(tc.tile_pool(name="cdp", bufs=2))
         outp = ctx.enter_context(tc.tile_pool(name="outp", bufs=3))
-        ptr = ctx.enter_context(tc.psum_pool(name="ptr", bufs=4))
-        pmm = ctx.enter_context(tc.psum_pool(name="pmm", bufs=4))
+        ptr = ctx.enter_context(tc.psum_pool(name="ptr", bufs=3))
+        pmm = ctx.enter_context(tc.psum_pool(name="pmm", bufs=5))
         ctx.enter_context(tc.manual_schedule())
 
         x = {}
@@ -161,7 +161,7 @@ def tile_generator_pb_kernel(tc, feat_gated, out):
             if h == 0:
                 grouped[c] = grp.tile([P, A, P, T], BF16, name="grouped", align_bytes=64)
             copy_out(
-                h == 1 and c >= 7,
+                h == 1 and c >= 6,
                 grouped[c][:, 2 * h:2 * h + 2, :, :].bitcast(F32),
                 xt[c, h][:].rearrange("p a u r -> p a r u"),
             )
@@ -185,7 +185,7 @@ def tile_generator_pb_kernel(tc, feat_gated, out):
             )
 
         def ev_on_vector(c, a):
-            return a % 2 == 1 and c >= 5
+            return (a % 2 == 1 and c >= 6) or (a == 3 and c >= 3)
 
         def evacuate(c, a):
             copy_out(
@@ -196,11 +196,9 @@ def tile_generator_pb_kernel(tc, feat_gated, out):
 
         def store(c):
             view = out[c].rearrange("(p a) n -> p a n", a=A)
-            if c >= NCOM - 3:
-                for a in range(A):
-                    nc.sync.dma_start(out=view[:, a, :], in_=osb[c][:, a, :])
-            else:
-                nc.sync.dma_start(out=view, in_=osb[c][:])
+            n = 1 if c >= NCOM - 3 else 2
+            for a in range(0, A, n):
+                nc.sync.dma_start(out=view[:, a:a + n, :], in_=osb[c][:, a:a + n, :])
 
         def scalar_stats(c):
             for a in range(A):
@@ -231,12 +229,14 @@ def tile_generator_pb_kernel(tc, feat_gated, out):
                 scalar_stats(p + 3)
             if ok(p + 2):
                 stats_through(p + 2)
+            if ok(p) and p >= 5:
+                quantise(p)
             if ok(p - 1):
                 osb[p - 1] = outp.tile([P, A, ROWS], F32, name="osb")
                 for a in range(A):
                     if ev_on_vector(p - 1, a):
                         evacuate(p - 1, a)
-            if ok(p):
+            if ok(p) and p < 5:
                 quantise(p)
             if ok(p + 2):
                 filler()

@@ -39,8 +39,9 @@ def tile_generator_pb_kernel(tc, feat_gated, out):
         grp = ctx.enter_context(tc.tile_pool(name="grp", bufs=2))
         cdp = ctx.enter_context(tc.tile_pool(name="cdp", bufs=2))
         outp = ctx.enter_context(tc.tile_pool(name="outp", bufs=3))
-        ptr = ctx.enter_context(tc.psum_pool(name="ptr", bufs=3))
+        ptr = ctx.enter_context(tc.psum_pool(name="ptr", bufs=2))
         pmm = ctx.enter_context(tc.psum_pool(name="pmm", bufs=5))
+        pkeep = ctx.enter_context(tc.psum_pool(name="pkeep", bufs=1))
         ctx.enter_context(tc.manual_schedule())
 
         x = {}
@@ -81,6 +82,11 @@ def tile_generator_pb_kernel(tc, feat_gated, out):
         nc.scalar.activation(out=warm[:], in_=warm[:], func=ACT.Abs_reciprocal_sqrt)
         ident = const.tile([P, P], F32, name="ident")
         masks.make_identity(nc, ident[:])
+        unread = pkeep.tile([P, P], F32, name="unread")
+
+        def keep_busy(n):
+            for i in range(n):
+                nc.tensor.matmul(unread[:], lhsT=ident[:], rhs=ident[:], start=True, stop=True)
 
         def unit():
             m = stream["next"]
@@ -150,6 +156,7 @@ def tile_generator_pb_kernel(tc, feat_gated, out):
                 words = fn[c][:, 2 * h + i, :].bitcast(F32)
                 for u in range(2):
                     nc.tensor.transpose(xt[c, h][:, i, u, :], words[:, u:2 * P:2], ident[:])
+            keep_busy(1)
 
         def copy_out(on_vector, dst, src_psum):
             if on_vector:
@@ -208,6 +215,7 @@ def tile_generator_pb_kernel(tc, feat_gated, out):
                 if stats_on_scalar(c, a):
                     scalar_sumsq(c, a)
 
+        keep_busy(8)
         scalar_stats(0)
         stats_through(0)
         root(0)

@@ -156,7 +156,8 @@ def tile_generator_pb_kernel(tc, feat_gated, out):
                 words = fn[c][:, 2 * h + i, :].bitcast(F32)
                 for u in range(2):
                     nc.tensor.transpose(xt[c, h][:, i, u, :], words[:, u:2 * P:2], ident[:])
-            keep_busy(1)
+            if h == 1 and c <= 5:
+                keep_busy(1)
 
         def copy_out(on_vector, dst, src_psum):
             if on_vector:
@@ -192,7 +193,7 @@ def tile_generator_pb_kernel(tc, feat_gated, out):
             )
 
         def ev_on_vector(c, a):
-            return (a % 2 == 1 and c >= 6) or (a == 3 and c >= 3)
+            return (a == 3 and c >= 3) or (a == 1 and c >= 6)
 
         def evacuate(c, a):
             copy_out(
@@ -203,7 +204,7 @@ def tile_generator_pb_kernel(tc, feat_gated, out):
 
         def store(c):
             view = out[c].rearrange("(p a) n -> p a n", a=A)
-            n = 1 if c >= NCOM - 3 else 2
+            n = 1 if c >= 4 else 2
             for a in range(0, A, n):
                 nc.sync.dma_start(out=view[:, a:a + n, :], in_=osb[c][:, a:a + n, :])
 
@@ -215,7 +216,7 @@ def tile_generator_pb_kernel(tc, feat_gated, out):
                 if stats_on_scalar(c, a):
                     scalar_sumsq(c, a)
 
-        keep_busy(8)
+        keep_busy(10)
         scalar_stats(0)
         stats_through(0)
         root(0)
@@ -253,7 +254,7 @@ def tile_generator_pb_kernel(tc, feat_gated, out):
                 for a in range(A):
                     if not ev_on_vector(p - 1, a):
                         evacuate(p - 1, a)
-                        if not rooted:
+                        if not rooted and a == 1:
                             root(p + 2)
                             rooted = True
             if not rooted:

@@ -193,7 +193,7 @@ def tile_generator_pb_kernel(tc, feat_gated, out):
             )
 
         def ev_on_vector(c, a):
-            return (a == 3 and c >= 3) or (a == 1 and c >= 6)
+            return (a == 1 and c >= 7) or (a == 3 and c >= 3)
 
         def evacuate(c, a):
             copy_out(
@@ -204,7 +204,7 @@ def tile_generator_pb_kernel(tc, feat_gated, out):
 
         def store(c):
             view = out[c].rearrange("(p a) n -> p a n", a=A)
-            n = 1 if c >= 4 else 2
+            n = 2
             for a in range(0, A, n):
                 nc.sync.dma_start(out=view[:, a:a + n, :], in_=osb[c][:, a:a + n, :])
 

@@ -69,11 +69,9 @@ def tile_generator_pb_kernel(tc, feat_gated, out):
         for c in range(NCOM):
             x[c] = xin.tile([P, A, K], BF16, name="x")
             src = feat_gated[c].rearrange("(p a) k -> p a k", a=A)
-            if c == 0:
-                for a in range(A):
-                    nc.sync.dma_start(out=x[c][:, a, :], in_=src[:, a, :])
-            else:
-                nc.sync.dma_start(out=x[c][:], in_=src)
+            n = 1 if c == 0 else 2 if c == 1 else A
+            for a in range(0, A, n):
+                nc.sync.dma_start(out=x[c][:, a:a + n, :], in_=src[:, a:a + n, :])
             st6[c] = small.tile([P, A, 6], F32, name="st6")
             mv[c] = small.tile([P, A, 2], F32, name="mv")
 
@@ -204,7 +202,7 @@ def tile_generator_pb_kernel(tc, feat_gated, out):
 
         def store(c):
             view = out[c].rearrange("(p a) n -> p a n", a=A)
-            n = 2
+            n = 1 if c in (3, 4) else 2
             for a in range(0, A, n):
                 nc.sync.dma_start(out=view[:, a:a + n, :], in_=osb[c][:, a:a + n, :])
 

from contextlib import ExitStack

import concourse.masks as masks
import concourse.mybir as mybir

BF16 = mybir.dt.bfloat16
F32 = mybir.dt.float32
U32 = mybir.dt.uint32
U8 = mybir.dt.uint8
FP8X4 = mybir.dt.float8_e4m3fn_x4
ALU = mybir.AluOpType
ACT = mybir.ActivationFunctionType

P = 128
NCOM = 8
ROWS = 512
K = 512
A = ROWS // P
T = K // P
FLOPS = 2 * NCOM * ROWS * ROWS * K


def stats_on_scalar(c, a):
    return a == 3 and c <= 3


def norm_on_gpsimd(c, a):
    return 2 <= c <= 6 and a >= 2


def tile_generator_pb_kernel(tc, feat_gated, out):
    nc = tc.nc
    with ExitStack() as ctx:
        const = ctx.enter_context(tc.tile_pool(name="const", bufs=1))
        xin = ctx.enter_context(tc.tile_pool(name="xin", bufs=NCOM))
        small = ctx.enter_context(tc.tile_pool(name="small", bufs=NCOM))
        junkp = ctx.enter_context(tc.tile_pool(name="junkp", bufs=2))
        fnp = ctx.enter_context(tc.tile_pool(name="fnp", bufs=4))
        grp = ctx.enter_context(tc.tile_pool(name="grp", bufs=2))
        cdp = ctx.enter_context(tc.tile_pool(name="cdp", bufs=2))
        outp = ctx.enter_context(tc.tile_pool(name="outp", bufs=3))
        ptr = ctx.enter_context(tc.psum_pool(name="ptr", bufs=2))
        pmm = ctx.enter_context(tc.psum_pool(name="pmm", bufs=5))
        pkeep = ctx.enter_context(tc.psum_pool(name="pkeep", bufs=1))
        ctx.enter_context(tc.manual_schedule())

        x = {}
        st6 = {}
        mv = {}
        smean = {}
        ssq = {}
        inv = {}
        fn = {}
        xt = {}
        grouped = {}
        codes = {}
        scales = {}
        acc = {}
        osb = {}
        stream = {"next": 0}
        vector_tiles = [(c, a) for c in range(NCOM) for a in range(A) if not stats_on_scalar(c, a)]
        last_of = {}
        for i, (c, a) in enumerate(vector_tiles):
            last_of[c] = i

        def ok(c):
            return 0 <= c < NCOM

        for c in range(NCOM):
            x[c] = xin.tile([P, A, K], BF16, name="x")
            src = feat_gated[c].rearrange("(p a) k -> p a k", a=A)
            n = 1 if c == 0 else 2 if c == 1 else A
            for a in range(0, A, n):
                nc.sync.dma_start(out=x[c][:, a:a + n, :], in_=src[:, a:a + n, :])
            st6[c] = small.tile([P, A, 6], F32, name="st6")
            mv[c] = small.tile([P, A, 2], F32, name="mv")

        warm = const.tile([P, 1], F32, name="warm")
        nc.vector.memset(warm[:], 1.0)
        nc.scalar.activation(out=warm[:], in_=warm[:], func=ACT.Abs_reciprocal_sqrt)
        ident = const.tile([P, P], F32, name="ident")
        masks.make_identity(nc, ident[:])
        unread = pkeep.tile([P, P], F32, name="unread")

        def keep_busy(n):
            for i in range(n):
                nc.tensor.matmul(unread[:], lhsT=ident[:], rhs=ident[:], start=True, stop=True)

        def unit():
            m = stream["next"]
            if m < len(vector_tiles):
                c, a = vector_tiles[m]
                nc.vector.bn_stats(out=st6[c][:, a, :], in_=x[c][:, a, :])
            if 1 <= m <= len(vector_tiles):
                c, a = vector_tiles[m - 1]
                nc.vector.bn_aggr(out=mv[c][:, a, :], in_=st6[c][:, a, :])
            stream["next"] = m + 1

        def stats_through(c):
            while stream["next"] <= last_of[c] + 1:
                unit()

        def filler():
            if stream["next"] <= len(vector_tiles):
                unit()

        def scalar_mean(c, a):
            smean[c, a] = small.tile([P, 1], F32, name="smean")
            junk = junkp.tile([P, K], BF16, name="junk")
            nc.scalar.activation(
                out=junk[:], in_=x[c][:, a, :], func=ACT.Identity, scale=1.0 / K, accum_out=smean[c, a][:]
            )

        def scalar_sumsq(c, a):
            ssq[c, a] = small.tile([P, 1], F32, name="ssq")
            junk = junkp.tile([P, K], BF16, name="junk")
            nc.scalar.activation(
                out=junk[:], in_=x[c][:, a, :], func=ACT.Square, scale=-1.0, bias=smean[c, a][:],
                accum_out=ssq[c, a][:],
            )

        def root(c):
            inv[c] = small.tile([P, A, 1], F32, name="inv")
            on_v = [a for a in range(A) if not stats_on_scalar(c, a)]
            lo, hi = on_v[0], on_v[-1] + 1
            nc.scalar.activation(out=inv[c][:, lo:hi, :], in_=mv[c][:, lo:hi, 1:2], func=ACT.Abs_reciprocal_sqrt, scale=float(K))
            for a in range(A):
                if stats_on_scalar(c, a):
                    nc.scalar.activation(out=inv[c][:, a, :], in_=ssq[c, a][:], func=ACT.Abs_reciprocal_sqrt)

        def normalise(c):
            fn[c] = fnp.tile([P, A, K], BF16, name="fn")
            for a in range(A):
                mean = smean[c, a][:] if stats_on_scalar(c, a) else mv[c][:, a, 0:1]
                if norm_on_gpsimd(c, a):
                    shift = small.tile([P, 1], F32, name="shift", bufs=4)
                    nc.gpsimd.tensor_scalar(
                        out=shift[:], in0=mean, scalar1=inv[c][:, a, :], scalar2=-1.0, op0=ALU.mult, op1=ALU.mult
                    )
                    nc.gpsimd.tensor_scalar(
                        out=fn[c][:, a, :], in0=x[c][:, a, :],
                        scalar1=inv[c][:, a, :], scalar2=shift[:], op0=ALU.mult, op1=ALU.add,
                    )
                else:
                    nc.vector.tensor_scalar(
                        out=fn[c][:, a, :], in0=x[c][:, a, :],
                        scalar1=mean, scalar2=inv[c][:, a, :],
                        op0=ALU.subtract, op1=ALU.mult,
                    )

        def transposes(c, h):
            xt[c, h] = ptr.tile([P, 2, 2, P], F32, name="xt")
            for i in range(2):
                words = fn[c][:, 2 * h + i, :].bitcast(F32)
                for u in range(2):
                    nc.tensor.transpose(xt[c, h][:, i, u, :], words[:, u:2 * P:2], ident[:])
            if h == 1 and c <= 5:
                keep_busy(1)

        def copy_out(on_vector, dst, src_psum):
            if on_vector:
                nc.vector.tensor_copy(out=dst, in_=src_psum)
            else:
                nc.scalar.copy(out=dst, in_=src_psum)

        def regroup(c, h):
            if h == 0:
                grouped[c] = grp.tile([P, A, P, T], BF16, name="grouped", align_bytes=64)
            copy_out(
                h == 1 and c >= 6,
                grouped[c][:, 2 * h:2 * h + 2, :, :].bitcast(F32),
                xt[c, h][:].rearrange("p a u r -> p a r u"),
            )

        def quantise(c):
            codes[c] = cdp.tile([P, ROWS], U32, name="codes", align_bytes=64)
            scales[c] = cdp.tile([P, ROWS], U8, name="scales", align_bytes=64)
            nc.vector.quantize_mx(
                out=codes[c][:].bitcast(FP8X4), scales=scales[c][:],
                in_=grouped[c][:].rearrange("p a r t -> p (a r t)"),
            )

        def product(c, a):
            acc[c, a] = pmm.tile([P, ROWS], F32, name="acc")
            cols = slice(a * P, (a + 1) * P)
            nc.tensor.matmul_mx(
                out=acc[c, a][:],
                lhsT=codes[c][:, cols].bitcast(FP8X4), lhsT_scale=scales[c][:, cols],
                rhs=codes[c][:].bitcast(FP8X4), rhs_scale=scales[c][:],
                start=True, stop=True,
            )

        def ev_on_vector(c, a):
            return (a == 1 and c >= 7) or (a == 3 and c >= 3)

        def evacuate(c, a):
            copy_out(
                ev_on_vector(c, a),
                osb[c][:, a, :].rearrange("p (r b) -> p r b", b=A),
                acc[c, a][:].rearrange("p (b r) -> p r b", b=A),
            )

        def store(c):
            view = out[c].rearrange("(p a) n -> p a n", a=A)
            n = 1 if c in (3, 4) else 2
            for a in range(0, A, n):
                nc.sync.dma_start(out=view[:, a:a + n, :], in_=osb[c][:, a:a + n, :])

        def scalar_stats(c):
            for a in range(A):
                if stats_on_scalar(c, a):
                    scalar_mean(c, a)
            for a in range(A):
                if stats_on_scalar(c, a):
                    scalar_sumsq(c, a)

        keep_busy(10)
        scalar_stats(0)
        stats_through(0)
        root(0)
        scalar_stats(1)
        scalar_stats(2)
        filler()
        filler()
        normalise(0)
        for h in range(2):
            transposes(0, h)

        for p in range(-1, NCOM + 1):
            if ok(p):
                for h in range(2):
                    regroup(p, h)
                    if ok(p + 1):
                        transposes(p + 1, h)
            if 0 <= p and ok(p + 3):
                scalar_stats(p + 3)
            if ok(p + 2):
                stats_through(p + 2)
            if ok(p) and p >= 5:
                quantise(p)
            if ok(p - 1):
                osb[p - 1] = outp.tile([P, A, ROWS], F32, name="osb")
                for a in range(A):
                    if ev_on_vector(p - 1, a):
                        evacuate(p - 1, a)
            if ok(p) and p < 5:
                quantise(p)
            if ok(p + 2):
                filler()
            rooted = not ok(p + 2)
            if ok(p - 1):
                for a in range(A):
                    if not ev_on_vector(p - 1, a):
                        evacuate(p - 1, a)
                        if not rooted and a == 1:
                            root(p + 2)
                            rooted = True
            if not rooted:
                root(p + 2)
            if ok(p - 1):
                store(p - 1)
            if ok(p + 2):
                filler()
                normalise(p + 2)
            if ok(p):
                for a in range(A):
                    product(p, a)
